import numpy as np
import ml_dtypes


def mxq(x, axis, fmt="e4m3"):
    dtype, down = {"e4m3": (ml_dtypes.float8_e4m3fn, 7), "e5m2": (ml_dtypes.float8_e5m2, 14)}[fmt]
    v = np.moveaxis(np.asarray(x, np.float32).astype(ml_dtypes.bfloat16).astype(np.float64), axis, -1)
    blocks = v.reshape(v.shape[:-1] + (-1, 32))
    amax = np.abs(blocks).max(-1, keepdims=True)
    byte = np.maximum(np.where(amax > 0, np.frexp(amax)[1] - 1 + 127, 0) - down, 1)
    scale = np.exp2(byte - 127.0)
    codes = (blocks / scale).astype(np.float32).astype(dtype).astype(np.float64)
    return np.moveaxis((codes * scale).reshape(v.shape), -1, axis)


WIDE = False


def mx_kscale(k):
    if not WIDE:
        return np.ones(k)
    levels = np.array([10, -10, 5, -5, 0])
    if k % 512:
        return np.exp2(np.random.permutation(np.resize(levels, k // 32))).repeat(32)
    a = np.empty((k // 512, 16))
    for p in range(k // 512):
        a[p, :8] = np.random.permutation(np.resize(levels, 8))
        for g in range(8):
            far = levels[np.abs(levels - a[p, g]) >= 10]
            a[p, g + 8] = far[np.random.randint(len(far))]
    return np.exp2(a.ravel()).repeat(32)


BF16 = ml_dtypes.bfloat16


def bf(x):
    return np.asarray(x, np.float32).astype(BF16)


def f64(x):
    return np.asarray(x).astype(np.float64)


B, IN, MEM, CTX, H, G = 512, 1024, 1024, 1024, 4, 3


def sigmoid(v):
    return 1.0 / (1.0 + np.exp(-v))


def setup_inputs():
    s = mx_kscale(IN)
    w = np.random.standard_normal((MEM, MEM + IN)) / np.sqrt(MEM + IN)
    w[:, MEM:] = w[:, MEM:] / s
    return {"input_tensor": bf(np.random.standard_normal((B, IN)) * s),
            "previous_memory": bf(np.random.standard_normal((B, MEM))),
            "fg_w": bf(w),
            "fg_b": bf(np.random.standard_normal(MEM) * 0.3)}


def reference(input_tensor, previous_memory, fg_w, fg_b):
    m = f64(previous_memory)
    forget_in = np.concatenate([m, f64(input_tensor)], axis=-1)
    fgate = sigmoid((mxq(forget_in, 1, "e4m3") @ mxq(f64(fg_w), 1, "e4m3").T) + f64(fg_b))
    return m * fgate

@@ -1,0 +1,186 @@
+from contextlib import ExitStack
+
+import concourse.mybir as mybir
+from concourse.masks import make_identity
+
+F32 = mybir.dt.float32
+BF16 = mybir.dt.bfloat16
+U32 = mybir.dt.uint32
+U8 = mybir.dt.uint8
+FP8X4 = mybir.dt.float8_e4m3fn_x4
+ADD = mybir.AluOpType.add
+MULT = mybir.AluOpType.mult
+SIGMOID = mybir.ActivationFunctionType.Sigmoid
+
+P = 128
+B, IN, MEM = 512, 1024, 1024
+K = MEM + IN
+FLOPS = 2 * B * MEM * K
+
+ROW_TILES = B // P
+GROUP = 256
+GROUPS = MEM // GROUP
+PASSES = K // (4 * P)
+WORDS = 2 * P
+PER_BANK = 4
+UNITS = 4
+
+STAGES = (("x", 0), ("w", 0), ("x", 1), ("w", 1), ("w", 2), ("w", 3))
+
+
+def output_banks(stage):
+    if stage < 0 or stage >= len(STAGES):
+        return []
+    kind, index = STAGES[stage]
+    seen = STAGES[:stage]
+    if kind == "x":
+        return [(q, index) for q in range(GROUPS) if ("w", q) in seen]
+    return [(index, h) for h in range(2) if ("x", h) in seen]
+
+
+def tile_dynamicmemorycell_pa_kernel(tc, input_tensor, previous_memory, fg_w, fg_b, out):
+    nc = tc.nc
+    with ExitStack() as ctx:
+        const = ctx.enter_context(tc.tile_pool(name="const", bufs=1))
+        keep = ctx.enter_context(tc.tile_pool(name="keep", bufs=1))
+        grouped_pool = ctx.enter_context(tc.tile_pool(name="grouped_pool", bufs=6))
+        gate_pool = ctx.enter_context(tc.tile_pool(name="gate_pool", bufs=4))
+        turned_pool = ctx.enter_context(tc.psum_pool(name="turned_pool", bufs=5))
+        acc_pool = ctx.enter_context(tc.psum_pool(name="acc_pool", bufs=3))
+        ctx.enter_context(tc.manual_schedule())
+
+        bias_row = const.tile([P, MEM], BF16, name="bias_row")
+        nc.vector.memset(bias_row[:], 0.0)
+        nc.scalar.dma_start(out=bias_row[0:1, :], in_=fg_b.unsqueeze(0))
+        ones = const.tile([P, P], BF16, name="ones")
+        nc.vector.memset(ones[:], 1.0)
+        zero_col = const.tile([P, 1], F32, name="zero_col")
+        nc.vector.memset(zero_col[:], 0.0)
+        half_col = const.tile([P, 1], F32, name="half_col")
+        nc.scalar.activation(out=half_col[:], in_=zero_col[:], func=SIGMOID)
+        ident = const.tile([P, P], F32, name="ident")
+        make_identity(nc, ident[:])
+        bias_all = const.tile([P, MEM], F32, name="bias_all")
+
+        x_dram = [a.rearrange("(p i) k -> p i k", i=ROW_TILES) for a in (previous_memory, input_tensor)]
+        x_sb = [keep.tile([P, ROW_TILES, MEM], BF16, name="x_sb%d" % s) for s in range(2)]
+        w_dram = fg_w.rearrange("(q c r) k -> q c r k", q=GROUPS, r=2)
+        w_sb = [keep.tile([P, 2, K], BF16, name="w_sb%d" % q) for q in range(GROUPS)]
+        out_dram = out.rearrange("(p i) n -> p i n", i=ROW_TILES)
+        for kind, index in STAGES:
+            if kind == "x":
+                rows = slice(2 * index, 2 * index + 2)
+                for s in range(2):
+                    nc.sync.dma_start(out=x_sb[s][:, rows, :], in_=x_dram[s][:, rows, :])
+            else:
+                nc.sync.dma_start(out=w_sb[index][:], in_=w_dram[index])
+
+        def operand_tiles(label, dtype, outer, inner):
+            return [
+                [keep.tile([P, GROUP], dtype, name="%s%d_%d" % (label, a, b), align_bytes=64) for b in range(inner)]
+                for a in range(outer)
+            ]
+
+        x_codes, x_scales = operand_tiles("x_codes", U32, 2, ROW_TILES), operand_tiles("x_scales", U8, 2, ROW_TILES)
+        w_codes, w_scales = operand_tiles("w_codes", U32, GROUPS, PASSES), operand_tiles("w_scales", U8, GROUPS, PASSES)
+
+        def transpose_unit(stage, unit):
+            kind, index = STAGES[stage]
+            turned = turned_pool.tile([P, PER_BANK, P], F32, name="turned")
+            for a in range(PER_BANK):
+                if kind == "x":
+                    words = x_sb[unit // 2][:, 2 * index + unit % 2, :].bitcast(F32)
+                    first = WORDS * (a // 2) + a % 2
+                else:
+                    words = w_sb[index][:, a // 2, :].bitcast(F32)
+                    first = WORDS * unit + a % 2
+                nc.tensor.transpose(turned[:, a, :], words[:, first : first + WORDS - 1 : 2], ident[:])
+            return turned
+
+        def copy_unit(stage, turned):
+            grouped = grouped_pool.tile([P, 4 * 2 * P], BF16, name="grouped", align_bytes=64)
+            if STAGES[stage][0] == "x":
+                dst = grouped[:].bitcast(F32).rearrange("p (g c u) -> p g c u", g=2, u=2)
+                src = turned[:].rearrange("p (g u) c -> p g c u", g=2)
+            else:
+                dst = grouped[:].bitcast(F32).rearrange("p (c a) -> p c a", a=PER_BANK)
+                src = turned[:].rearrange("p a c -> p c a")
+            nc.scalar.copy(out=dst, in_=src)
+            return grouped
+
+        def quantise_unit(stage, unit, grouped):
+            kind, index = STAGES[stage]
+            if kind == "x":
+                codes, scales = x_codes[unit // 2][2 * index + unit % 2], x_scales[unit // 2][2 * index + unit % 2]
+            else:
+                codes, scales = w_codes[index][unit], w_scales[index][unit]
+            nc.vector.quantize_mx(out=codes[:].bitcast(FP8X4), scales=scales[:], in_=grouped[:])
+
+        def spread_bias():
+            for half in range(2):
+                cols = slice(512 * half, 512 * (half + 1))
+                spread = acc_pool.tile([P, 512], F32, name="spread", tag="acc")
+                nc.tensor.matmul(out=spread[:], lhsT=ones[:], rhs=bias_row[:, cols], start=True, stop=True)
+                nc.vector.tensor_copy(out=bias_all[:, cols], in_=spread[:])
+
+        def multiply(bank):
+            q, h = bank
+            acc = acc_pool.tile([P, 2, GROUP], F32, name="acc", tag="acc")
+            for j in range(2):
+                i = 2 * h + j
+                for g in range(PASSES):
+                    cols = slice(P * (g % 2), P * (g % 2 + 1))
+                    nc.tensor.matmul_mx(
+                        out=acc[:, j, :],
+                        lhsT=x_codes[g // 2][i][:, cols].bitcast(FP8X4),
+                        lhsT_scale=x_scales[g // 2][i][:, cols],
+                        rhs=w_codes[q][g][:].bitcast(FP8X4),
+                        rhs_scale=w_scales[q][g][:],
+                        start=(g == 0),
+                        stop=(g == PASSES - 1),
+                    )
+            return acc
+
+        def add_bias(bank, acc):
+            cols = slice(GROUP * bank[0], GROUP * (bank[0] + 1))
+            logits = gate_pool.tile([P, 2, GROUP], F32, name="logits")
+            nc.vector.tensor_tensor(
+                out=logits[:], in0=acc[:], in1=bias_all[:, cols].unsqueeze(1).to_broadcast([P, 2, GROUP]), op=ADD
+            )
+            return logits
+
+        def squash(logits):
+            gate = gate_pool.tile([P, 2, GROUP], F32, name="gate")
+            nc.scalar.activation(out=gate[:], in_=logits[:], func=SIGMOID)
+            return gate
+
+        def finish(bank, gate, engine):
+            q, h = bank
+            rows, cols = slice(2 * h, 2 * h + 2), slice(GROUP * q, GROUP * (q + 1))
+            result = gate_pool.tile([P, 2, GROUP], F32, name="result")
+            engine.tensor_tensor(out=result[:], in0=gate[:], in1=x_sb[0][:, rows, cols], op=MULT)
+            nc.sync.dma_start(out=out_dram[:, rows, cols], in_=result[:])
+
+        accs, logit_tiles, gates = {}, {}, {}
+        for r in range(-1, len(STAGES) + 2):
+            units = range(UNITS) if r + 1 < len(STAGES) else []
+            turned = [transpose_unit(r + 1, unit) for unit in units]
+            for bank in output_banks(r - 1):
+                logit_tiles[bank] = add_bias(bank, accs[bank])
+            last = output_banks(r - 2)
+            grouped = []
+            for unit in units:
+                grouped.append(copy_unit(r + 1, turned[unit]))
+                if unit > 0:
+                    quantise_unit(r + 1, unit - 1, grouped[unit - 1])
+            for bank in last:
+                shared = len(last) == 2 and bank == last[0] and len(output_banks(r - 1)) > 0
+                finish(bank, gates[bank], nc.gpsimd if shared else nc.vector)
+            for bank in output_banks(r - 1):
+                gates[bank] = squash(logit_tiles[bank])
+            if grouped:
+                quantise_unit(r + 1, UNITS - 1, grouped[UNITS - 1])
+            if r == 0:
+                spread_bias()
+            for bank in output_banks(r):
+                accs[bank] = multiply(bank)

@@ -50,8 +50,7 @@ def tile_dynamicmemorycell_pa_kernel(tc, input_tensor, previous_memory, fg_w, fg
         ctx.enter_context(tc.manual_schedule())
 
         bias_row = const.tile([P, MEM], BF16, name="bias_row")
-        nc.vector.memset(bias_row[:], 0.0)
-        nc.scalar.dma_start(out=bias_row[0:1, :], in_=fg_b.unsqueeze(0))
+        nc.gpsimd.memset(bias_row[:].bitcast(F32), 0.0)
         ones = const.tile([P, P], BF16, name="ones")
         nc.vector.memset(ones[:], 1.0)
         zero_col = const.tile([P, 1], F32, name="zero_col")
@@ -71,7 +70,13 @@ def tile_dynamicmemorycell_pa_kernel(tc, input_tensor, previous_memory, fg_w, fg
             if kind == "x":
                 rows = slice(2 * index, 2 * index + 2)
                 for s in range(2):
-                    nc.sync.dma_start(out=x_sb[s][:, rows, :], in_=x_dram[s][:, rows, :])
+                    if index == 0:
+                        for i in range(2):
+                            nc.sync.dma_start(out=x_sb[s][:, i, :], in_=x_dram[s][:, i, :])
+                            if s == 0 and i == 0:
+                                nc.sync.dma_start(out=bias_row[0:1, :], in_=fg_b.unsqueeze(0))
+                    else:
+                        nc.sync.dma_start(out=x_sb[s][:, rows, :], in_=x_dram[s][:, rows, :])
             else:
                 nc.sync.dma_start(out=w_sb[index][:], in_=w_dram[index])
 
@@ -180,7 +185,7 @@ def tile_dynamicmemorycell_pa_kernel(tc, input_tensor, previous_memory, fg_w, fg
                 gates[bank] = squash(logit_tiles[bank])
             if grouped:
                 quantise_unit(r + 1, UNITS - 1, grouped[UNITS - 1])
-            if r == 0:
+            if r == -1:
                 spread_bias()
             for bank in output_banks(r):
                 accs[bank] = multiply(bank)

@@ -23,6 +23,7 @@ GROUPS = MEM // GROUP
 PASSES = K // (4 * P)
 WORDS = 2 * P
 PER_BANK = 4
+FIRST_SORTED = 2
 UNITS = 4
 
 STAGES = (("x", 0), ("w", 0), ("x", 1), ("w", 1), ("w", 2), ("w", 3))
@@ -44,6 +45,7 @@ def tile_dynamicmemorycell_pa_kernel(tc, input_tensor, previous_memory, fg_w, fg
         const = ctx.enter_context(tc.tile_pool(name="const", bufs=1))
         keep = ctx.enter_context(tc.tile_pool(name="keep", bufs=1))
         grouped_pool = ctx.enter_context(tc.tile_pool(name="grouped_pool", bufs=6))
+        sorted_pool = ctx.enter_context(tc.tile_pool(name="sorted_pool", bufs=2 * UNITS))
         gate_pool = ctx.enter_context(tc.tile_pool(name="gate_pool", bufs=4))
         turned_pool = ctx.enter_context(tc.psum_pool(name="turned_pool", bufs=5))
         acc_pool = ctx.enter_context(tc.psum_pool(name="acc_pool", bufs=3))
@@ -89,10 +91,25 @@ def tile_dynamicmemorycell_pa_kernel(tc, input_tensor, previous_memory, fg_w, fg
         x_codes, x_scales = operand_tiles("x_codes", U32, 2, ROW_TILES), operand_tiles("x_scales", U8, 2, ROW_TILES)
         w_codes, w_scales = operand_tiles("w_codes", U32, GROUPS, PASSES), operand_tiles("w_scales", U8, GROUPS, PASSES)
 
-        def transpose_unit(stage, unit):
+        def sort_unit(stage, unit):
+            kind, index = STAGES[stage]
+            parity = sorted_pool.tile([P, PER_BANK, P], F32, name="parity")
+            dst = parity[:].rearrange("p (b u) c -> p b u c", u=2)
+            if kind == "x":
+                src = x_sb[unit // 2][:, 2 * index + unit % 2, :].bitcast(F32).rearrange("p (b c u) -> p b u c", b=2, u=2)
+            else:
+                src = w_sb[index][:, :, 2 * WORDS * unit : 2 * WORDS * (unit + 1)].bitcast(F32)
+                src = src.rearrange("p b (c u) -> p b u c", u=2)
+            nc.vector.tensor_copy(out=dst, in_=src)
+            return parity
+
+        def transpose_unit(stage, unit, parity):
             kind, index = STAGES[stage]
             turned = turned_pool.tile([P, PER_BANK, P], F32, name="turned")
             for a in range(PER_BANK):
+                if parity is not None:
+                    nc.tensor.transpose(turned[:, a, :], parity[:, a, :], ident[:])
+                    continue
                 if kind == "x":
                     words = x_sb[unit // 2][:, 2 * index + unit % 2, :].bitcast(F32)
                     first = WORDS * (a // 2) + a % 2
@@ -167,15 +184,18 @@ def tile_dynamicmemorycell_pa_kernel(tc, input_tensor, previous_memory, fg_w, fg
             nc.sync.dma_start(out=out_dram[:, rows, cols], in_=result[:])
 
         accs, logit_tiles, gates = {}, {}, {}
+        sorted_units = {}
         for r in range(-1, len(STAGES) + 2):
             units = range(UNITS) if r + 1 < len(STAGES) else []
-            turned = [transpose_unit(r + 1, unit) for unit in units]
+            turned = [transpose_unit(r + 1, unit, sorted_units.get((r + 1, unit))) for unit in units]
             for bank in output_banks(r - 1):
                 logit_tiles[bank] = add_bias(bank, accs[bank])
             last = output_banks(r - 2)
             grouped = []
             for unit in units:
                 grouped.append(copy_unit(r + 1, turned[unit]))
+                if FIRST_SORTED <= r + 2 < len(STAGES):
+                    sorted_units[(r + 2, unit)] = sort_unit(r + 2, unit)
                 if unit > 0:
                     quantise_unit(r + 1, unit - 1, grouped[unit - 1])
             for bank in last:

@@ -52,7 +52,7 @@ def tile_dynamicmemorycell_pa_kernel(tc, input_tensor, previous_memory, fg_w, fg
         ctx.enter_context(tc.manual_schedule())
 
         bias_row = const.tile([P, MEM], BF16, name="bias_row")
-        nc.gpsimd.memset(bias_row[:].bitcast(F32), 0.0)
+        nc.vector.memset(bias_row[:].bitcast(F32), 0.0)
         ones = const.tile([P, P], BF16, name="ones")
         nc.vector.memset(ones[:], 1.0)
         zero_col = const.tile([P, 1], F32, name="zero_col")
@@ -72,13 +72,9 @@ def tile_dynamicmemorycell_pa_kernel(tc, input_tensor, previous_memory, fg_w, fg
             if kind == "x":
                 rows = slice(2 * index, 2 * index + 2)
                 for s in range(2):
-                    if index == 0:
-                        for i in range(2):
-                            nc.sync.dma_start(out=x_sb[s][:, i, :], in_=x_dram[s][:, i, :])
-                            if s == 0 and i == 0:
-                                nc.sync.dma_start(out=bias_row[0:1, :], in_=fg_b.unsqueeze(0))
-                    else:
-                        nc.sync.dma_start(out=x_sb[s][:, rows, :], in_=x_dram[s][:, rows, :])
+                    nc.sync.dma_start(out=x_sb[s][:, rows, :], in_=x_dram[s][:, rows, :])
+                if index == 0:
+                    nc.sync.dma_start(out=bias_row[0:1, :], in_=fg_b.unsqueeze(0))
             else:
                 nc.sync.dma_start(out=w_sb[index][:], in_=w_dram[index])
 
@@ -205,7 +201,7 @@ def tile_dynamicmemorycell_pa_kernel(tc, input_tensor, previous_memory, fg_w, fg
                 gates[bank] = squash(logit_tiles[bank])
             if grouped:
                 quantise_unit(r + 1, UNITS - 1, grouped[UNITS - 1])
-            if r == -1:
+            if r == 0:
                 spread_bias()
             for bank in output_banks(r):
                 accs[bank] = multiply(bank)

from contextlib import ExitStack

import concourse.mybir as mybir
from concourse.masks import make_identity

F32 = mybir.dt.float32
BF16 = mybir.dt.bfloat16
U32 = mybir.dt.uint32
U8 = mybir.dt.uint8
FP8X4 = mybir.dt.float8_e4m3fn_x4
ADD = mybir.AluOpType.add
MULT = mybir.AluOpType.mult
SIGMOID = mybir.ActivationFunctionType.Sigmoid

P = 128
B, IN, MEM = 512, 1024, 1024
K = MEM + IN
FLOPS = 2 * B * MEM * K

ROW_TILES = B // P
GROUP = 256
GROUPS = MEM // GROUP
PASSES = K // (4 * P)
WORDS = 2 * P
PER_BANK = 4
FIRST_SORTED = 2
UNITS = 4

STAGES = (("x", 0), ("w", 0), ("x", 1), ("w", 1), ("w", 2), ("w", 3))


def output_banks(stage):
    if stage < 0 or stage >= len(STAGES):
        return []
    kind, index = STAGES[stage]
    seen = STAGES[:stage]
    if kind == "x":
        return [(q, index) for q in range(GROUPS) if ("w", q) in seen]
    return [(index, h) for h in range(2) if ("x", h) in seen]


def tile_dynamicmemorycell_pa_kernel(tc, input_tensor, previous_memory, fg_w, fg_b, out):
    nc = tc.nc
    with ExitStack() as ctx:
        const = ctx.enter_context(tc.tile_pool(name="const", bufs=1))
        keep = ctx.enter_context(tc.tile_pool(name="keep", bufs=1))
        grouped_pool = ctx.enter_context(tc.tile_pool(name="grouped_pool", bufs=6))
        sorted_pool = ctx.enter_context(tc.tile_pool(name="sorted_pool", bufs=2 * UNITS))
        gate_pool = ctx.enter_context(tc.tile_pool(name="gate_pool", bufs=4))
        turned_pool = ctx.enter_context(tc.psum_pool(name="turned_pool", bufs=5))
        acc_pool = ctx.enter_context(tc.psum_pool(name="acc_pool", bufs=3))
        ctx.enter_context(tc.manual_schedule())

        bias_row = const.tile([P, MEM], BF16, name="bias_row")
        nc.vector.memset(bias_row[:].bitcast(F32), 0.0)
        ones = const.tile([P, P], BF16, name="ones")
        nc.vector.memset(ones[:], 1.0)
        zero_col = const.tile([P, 1], F32, name="zero_col")
        nc.vector.memset(zero_col[:], 0.0)
        half_col = const.tile([P, 1], F32, name="half_col")
        nc.scalar.activation(out=half_col[:], in_=zero_col[:], func=SIGMOID)
        ident = const.tile([P, P], F32, name="ident")
        make_identity(nc, ident[:])
        bias_all = const.tile([P, MEM], F32, name="bias_all")

        x_dram = [a.rearrange("(p i) k -> p i k", i=ROW_TILES) for a in (previous_memory, input_tensor)]
        x_sb = [keep.tile([P, ROW_TILES, MEM], BF16, name="x_sb%d" % s) for s in range(2)]
        w_dram = fg_w.rearrange("(q c r) k -> q c r k", q=GROUPS, r=2)
        w_sb = [keep.tile([P, 2, K], BF16, name="w_sb%d" % q) for q in range(GROUPS)]
        out_dram = out.rearrange("(p i) n -> p i n", i=ROW_TILES)
        for kind, index in STAGES:
            if kind == "x":
                rows = slice(2 * index, 2 * index + 2)
                for s in range(2):
                    nc.sync.dma_start(out=x_sb[s][:, rows, :], in_=x_dram[s][:, rows, :])
                if index == 0:
                    nc.sync.dma_start(out=bias_row[0:1, :], in_=fg_b.unsqueeze(0))
            else:
                nc.sync.dma_start(out=w_sb[index][:], in_=w_dram[index])

        def operand_tiles(label, dtype, outer, inner):
            return [
                [keep.tile([P, GROUP], dtype, name="%s%d_%d" % (label, a, b), align_bytes=64) for b in range(inner)]
                for a in range(outer)
            ]

        x_codes, x_scales = operand_tiles("x_codes", U32, 2, ROW_TILES), operand_tiles("x_scales", U8, 2, ROW_TILES)
        w_codes, w_scales = operand_tiles("w_codes", U32, GROUPS, PASSES), operand_tiles("w_scales", U8, GROUPS, PASSES)

        def sort_unit(stage, unit):
            kind, index = STAGES[stage]
            parity = sorted_pool.tile([P, PER_BANK, P], F32, name="parity")
            dst = parity[:].rearrange("p (b u) c -> p b u c", u=2)
            if kind == "x":
                src = x_sb[unit // 2][:, 2 * index + unit % 2, :].bitcast(F32).rearrange("p (b c u) -> p b u c", b=2, u=2)
            else:
                src = w_sb[index][:, :, 2 * WORDS * unit : 2 * WORDS * (unit + 1)].bitcast(F32)
                src = src.rearrange("p b (c u) -> p b u c", u=2)
            nc.vector.tensor_copy(out=dst, in_=src)
            return parity

        def transpose_unit(stage, unit, parity):
            kind, index = STAGES[stage]
            turned = turned_pool.tile([P, PER_BANK, P], F32, name="turned")
            for a in range(PER_BANK):
                if parity is not None:
                    nc.tensor.transpose(turned[:, a, :], parity[:, a, :], ident[:])
                    continue
                if kind == "x":
                    words = x_sb[unit // 2][:, 2 * index + unit % 2, :].bitcast(F32)
                    first = WORDS * (a // 2) + a % 2
                else:
                    words = w_sb[index][:, a // 2, :].bitcast(F32)
                    first = WORDS * unit + a % 2
                nc.tensor.transpose(turned[:, a, :], words[:, first : first + WORDS - 1 : 2], ident[:])
            return turned

        def copy_unit(stage, turned):
            grouped = grouped_pool.tile([P, 4 * 2 * P], BF16, name="grouped", align_bytes=64)
            if STAGES[stage][0] == "x":
                dst = grouped[:].bitcast(F32).rearrange("p (g c u) -> p g c u", g=2, u=2)
                src = turned[:].rearrange("p (g u) c -> p g c u", g=2)
            else:
                dst = grouped[:].bitcast(F32).rearrange("p (c a) -> p c a", a=PER_BANK)
                src = turned[:].rearrange("p a c -> p c a")
            nc.scalar.copy(out=dst, in_=src)
            return grouped

        def quantise_unit(stage, unit, grouped):
            kind, index = STAGES[stage]
            if kind == "x":
                codes, scales = x_codes[unit // 2][2 * index + unit % 2], x_scales[unit // 2][2 * index + unit % 2]
            else:
                codes, scales = w_codes[index][unit], w_scales[index][unit]
            nc.vector.quantize_mx(out=codes[:].bitcast(FP8X4), scales=scales[:], in_=grouped[:])

        def spread_bias():
            for half in range(2):
                cols = slice(512 * half, 512 * (half + 1))
                spread = acc_pool.tile([P, 512], F32, name="spread", tag="acc")
                nc.tensor.matmul(out=spread[:], lhsT=ones[:], rhs=bias_row[:, cols], start=True, stop=True)
                nc.vector.tensor_copy(out=bias_all[:, cols], in_=spread[:])

        def multiply(bank):
            q, h = bank
            acc = acc_pool.tile([P, 2, GROUP], F32, name="acc", tag="acc")
            for j in range(2):
                i = 2 * h + j
                for g in range(PASSES):
                    cols = slice(P * (g % 2), P * (g % 2 + 1))
                    nc.tensor.matmul_mx(
                        out=acc[:, j, :],
                        lhsT=x_codes[g // 2][i][:, cols].bitcast(FP8X4),
                        lhsT_scale=x_scales[g // 2][i][:, cols],
                        rhs=w_codes[q][g][:].bitcast(FP8X4),
                        rhs_scale=w_scales[q][g][:],
                        start=(g == 0),
                        stop=(g == PASSES - 1),
                    )
            return acc

        def add_bias(bank, acc):
            cols = slice(GROUP * bank[0], GROUP * (bank[0] + 1))
            logits = gate_pool.tile([P, 2, GROUP], F32, name="logits")
            nc.vector.tensor_tensor(
                out=logits[:], in0=acc[:], in1=bias_all[:, cols].unsqueeze(1).to_broadcast([P, 2, GROUP]), op=ADD
            )
            return logits

        def squash(logits):
            gate = gate_pool.tile([P, 2, GROUP], F32, name="gate")
            nc.scalar.activation(out=gate[:], in_=logits[:], func=SIGMOID)
            return gate

        def finish(bank, gate, engine):
            q, h = bank
            rows, cols = slice(2 * h, 2 * h + 2), slice(GROUP * q, GROUP * (q + 1))
            result = gate_pool.tile([P, 2, GROUP], F32, name="result")
            engine.tensor_tensor(out=result[:], in0=gate[:], in1=x_sb[0][:, rows, cols], op=MULT)
            nc.sync.dma_start(out=out_dram[:, rows, cols], in_=result[:])

        accs, logit_tiles, gates = {}, {}, {}
        sorted_units = {}
        for r in range(-1, len(STAGES) + 2):
            units = range(UNITS) if r + 1 < len(STAGES) else []
            turned = [transpose_unit(r + 1, unit, sorted_units.get((r + 1, unit))) for unit in units]
            for bank in output_banks(r - 1):
                logit_tiles[bank] = add_bias(bank, accs[bank])
            last = output_banks(r - 2)
            grouped = []
            for unit in units:
                grouped.append(copy_unit(r + 1, turned[unit]))
                if FIRST_SORTED <= r + 2 < len(STAGES):
                    sorted_units[(r + 2, unit)] = sort_unit(r + 2, unit)
                if unit > 0:
                    quantise_unit(r + 1, unit - 1, grouped[unit - 1])
            for bank in last:
                shared = len(last) == 2 and bank == last[0] and len(output_banks(r - 1)) > 0
                finish(bank, gates[bank], nc.gpsimd if shared else nc.vector)
            for bank in output_banks(r - 1):
                gates[bank] = squash(logit_tiles[bank])
            if grouped:
                quantise_unit(r + 1, UNITS - 1, grouped[UNITS - 1])
            if r == 0:
                spread_bias()
            for bank in output_banks(r):
                accs[bank] = multiply(bank)
